import numpy as np
import ml_dtypes


def mxq(x, axis, fmt="e4m3"):
    dtype, down = {"e4m3": (ml_dtypes.float8_e4m3fn, 7), "e5m2": (ml_dtypes.float8_e5m2, 14)}[fmt]
    v = np.moveaxis(np.asarray(x, np.float32).astype(ml_dtypes.bfloat16).astype(np.float64), axis, -1)
    blocks = v.reshape(v.shape[:-1] + (-1, 32))
    amax = np.abs(blocks).max(-1, keepdims=True)
    byte = np.maximum(np.where(amax > 0, np.frexp(amax)[1] - 1 + 127, 0) - down, 1)
    scale = np.exp2(byte - 127.0)
    codes = (blocks / scale).astype(np.float32).astype(dtype).astype(np.float64)
    return np.moveaxis((codes * scale).reshape(v.shape), -1, axis)


WIDE = False


def mx_kscale(k):
    if not WIDE:
        return np.ones(k)
    levels = np.array([10, -10, 5, -5, 0])
    if k % 512:
        return np.exp2(np.random.permutation(np.resize(levels, k // 32))).repeat(32)
    a = np.empty((k // 512, 16))
    for p in range(k // 512):
        a[p, :8] = np.random.permutation(np.resize(levels, 8))
        for g in range(8):
            far = levels[np.abs(levels - a[p, g]) >= 10]
            a[p, g + 8] = far[np.random.randint(len(far))]
    return np.exp2(a.ravel()).repeat(32)


BF16 = ml_dtypes.bfloat16


def bf(x):
    return np.asarray(x, np.float32).astype(BF16)


def f64(x):
    return np.asarray(x).astype(np.float64)


E2M1 = np.array([0.0, 0.5, 1.0, 1.5, 2.0, 3.0, 4.0, 6.0, -0.0, -0.5, -1.0, -1.5, -2.0, -3.0, -4.0, -6.0])


def pack_weight(w, fmt):
    k, n = w.shape
    w = f64(bf(w)).reshape(k // 32, 32, n)
    amax = np.abs(w).max(1)
    if fmt == "e4m3":
        byte = np.frexp(amax)[1] - 1 + 127 - 7
    else:
        mant, ex = np.frexp(amax / 6.0)
        byte = np.where(mant > 0.5, ex, ex - 1) + 127
    byte = np.clip(np.where(amax > 0, byte, 1), 1, 254)
    scaled = (w * np.exp2(127.0 - byte)[:, None, :]).reshape(k, n).astype(np.float32)
    by_word = np.ascontiguousarray(scaled.reshape(k // 512, 128, 4, n).transpose(0, 1, 3, 2))
    if fmt == "e4m3":
        words = by_word.astype(ml_dtypes.float8_e4m3fn).view(np.uint8)
    else:
        c = by_word.astype(ml_dtypes.float4_e2m1fn).view(np.uint8) & 0xF
        words = c[..., 0::2] | (c[..., 1::2] << 4)
    return np.ascontiguousarray(words), np.ascontiguousarray(byte.astype(np.uint8).reshape(k // 512, 16, n))


def unpack_weight(words, scales, fmt):
    g, p, n, _ = words.shape
    if fmt == "e4m3":
        vals = np.ascontiguousarray(words).view(ml_dtypes.float8_e4m3fn).astype(np.float64)
    else:
        nib = np.empty((g, p, n, 4), np.uint8)
        nib[..., 0::2] = words & 0xF
        nib[..., 1::2] = words >> 4
        vals = E2M1[nib]
    vals = vals * np.repeat(np.exp2(scales.astype(np.float64) - 127.0), 8, axis=1)[..., None]
    return vals.transpose(0, 1, 3, 2).reshape(g * 512, n)


B, T, DX, DY, F = 128, 8, 1024, 1024, 5
MIN_CONTEXT = 1
G = 1.5 / DY ** 0.25


def setup_inputs():
    s, t = mx_kscale(DX), mx_kscale(DY)
    embeddings = bf(np.random.standard_normal((B, T, DX)) * s)
    contexts = bf(np.random.standard_normal((B, T, DY)) * G / t)
    stack = (np.random.standard_normal((F, DY, DX)) * G / np.sqrt(DX) * t[:, None] / s).swapaxes(1, 2)
    words, scales = pack_weight(stack.reshape(-1, DY), "e4m3")
    return {"embeddings": embeddings,
            "contexts": contexts,
            "W_words": words,
            "W_scales": scales}


def reference(embeddings, contexts, W_words, W_scales):
    eq = mxq(f64(embeddings)[:, MIN_CONTEXT:T], 2, "e4m3")
    cq = mxq(f64(contexts)[:, MIN_CONTEXT - 1:T - 1], 2, "e4m3")
    wq = unpack_weight(W_words, W_scales, "e4m3").reshape(F, DX, DY)
    losses = []
    for step in range(F):
        S = T - step - MIN_CONTEXT
        xw = eq[:, step:] @ wq[step]
        scores = mxq(xw, 2, "e4m3").transpose(1, 0, 2) @ cq[:, :S].transpose(1, 2, 0)
        pos = np.diagonal(scores, axis1=1, axis2=2)
        m = scores.max(2, keepdims=True)
        lse = np.log(np.exp(scores - m).sum(2)) + m[:, :, 0] - np.log(B * S)
        losses.append((lse - pos).T.reshape(-1))
    return np.concatenate(losses)

@@ -1,0 +1,320 @@
+import math
+from contextlib import ExitStack
+
+import concourse.mybir as mybir
+from concourse.masks import make_identity
+
+F32 = mybir.dt.float32
+BF16 = mybir.dt.bfloat16
+I32 = mybir.dt.int32
+U32 = mybir.dt.uint32
+U8 = mybir.dt.uint8
+FP8X4 = mybir.dt.float8_e4m3fn_x4
+ALU = mybir.AluOpType
+ACT = mybir.ActivationFunctionType
+AXIS_X = mybir.AxisListType.X
+
+P = 128
+T = 8
+N_SLICES = T - 1
+D = 1024
+STEPS = 5
+PACK = 4
+K_PASS = P * PACK
+PASSES = D // K_PASS
+PLANES_PER_SLOT = 4
+QUADRANT = 32
+SLICES_PER_LOAD = 2
+ROWS_PER_GROUP = 8
+GROUPS = P // ROWS_PER_GROUP
+QUANTISE_LAG = 1
+COMPARE_LAG = 3
+EXP_LAG = 4
+ORDER_LEAD = 4
+
+N_PAIRS = sum(N_SLICES - step for step in range(STEPS))
+FLOPS = 2 * N_PAIRS * P * D * D + 2 * N_PAIRS * P * P * D
+
+
+def tile_infonceloss_pa_e_kernel(tc, embeddings, contexts, W_words, W_scales, out):
+    nc = tc.nc
+    pairs = [(step, s) for step in range(STEPS) for s in range(N_SLICES - step)]
+    first_pair = [pairs.index((step, 0)) for step in range(STEPS)]
+
+    with ExitStack() as ctx:
+        keep = ctx.enter_context(tc.tile_pool(name="keep", bufs=1))
+        slice_stage = ctx.enter_context(tc.tile_pool(name="slice_stage", bufs=4))
+        xw_stage = ctx.enter_context(tc.tile_pool(name="xw_stage", bufs=3))
+        unread = ctx.enter_context(tc.tile_pool(name="unread", bufs=4))
+        psum_banks = ctx.enter_context(tc.psum_pool(name="psum_banks", bufs=6))
+        psum_scores = ctx.enter_context(tc.psum_pool(name="psum_scores", bufs=2))
+        ctx.enter_context(tc.manual_schedule())
+
+        e_raw = keep.tile([P, N_SLICES, D], BF16)
+        c_raw = keep.tile([P, N_SLICES, D], BF16)
+        w_words = keep.tile([P, STEPS, PASSES, D], U32, align_bytes=64)
+        n_planes = STEPS * PASSES
+        n_slots = (n_planes + PLANES_PER_SLOT - 1) // PLANES_PER_SLOT
+        w_planes = keep.tile([P, n_slots, D], U8, align_bytes=64)
+        raw_words = keep.tile([P, STEPS, PASSES, D], U32, align_bytes=64)
+        raw_planes = keep.tile([P, n_slots, D], U8, align_bytes=64)
+        e_words = keep.tile([P, N_SLICES, PASSES, P], U32, align_bytes=64)
+        e_scales = keep.tile([P, N_SLICES, PASSES, P], U8, align_bytes=64)
+        c_words = keep.tile([P, N_SLICES, PASSES, P], U32, align_bytes=64)
+        c_scales = keep.tile([P, N_SLICES, PASSES, P], U8, align_bytes=64)
+        xw_words = keep.tile([P, N_PAIRS, PASSES, P], U32, align_bytes=64)
+        xw_scales = keep.tile([P, N_PAIRS, PASSES, P], U8, align_bytes=64)
+        neg_max = keep.tile([P, N_PAIRS], F32)
+        sum_exp = keep.tile([P, N_PAIRS], F32)
+        diagonal = keep.tile([P, N_PAIRS], F32)
+        shift = keep.tile([P, N_PAIRS], F32)
+        spread_sum = keep.tile([P, ROWS_PER_GROUP * N_PAIRS], F32)
+        spread_shift = keep.tile([P, ROWS_PER_GROUP * N_PAIRS], F32)
+
+        nc.vector.memset(raw_planes[:].bitcast(I32), 0)
+
+        def load_slices(lo, hi):
+            nc.sync.dma_start(out=e_raw[:, lo:hi, :], in_=embeddings[:, 1 + lo : 1 + hi, :])
+            nc.sync.dma_start(out=c_raw[:, lo:hi, :], in_=contexts[:, lo:hi, :])
+
+        def load_scale_slot(slot):
+            lo = PLANES_PER_SLOT * slot
+            hi = min(lo + PLANES_PER_SLOT, n_planes)
+            for quadrant in range(P // QUADRANT):
+                top = QUADRANT * quadrant
+                nc.sync.dma_start(
+                    out=raw_planes[top : top + 4 * (hi - lo), slot, :].bitcast(I32),
+                    in_=W_scales[lo:hi, 4 * quadrant : 4 * quadrant + 4, :].bitcast(I32),
+                )
+
+        def load_weight(step, lo, hi):
+            nc.sync.dma_start(
+                out=raw_words[:, step, :, lo:hi].bitcast(I32),
+                in_=W_words[PASSES * step : PASSES * (step + 1)]
+                .rearrange("g p n t -> p g (n t)")[:, :, PACK * lo : PACK * hi]
+                .bitcast(I32),
+            )
+
+        load_slices(0, SLICES_PER_LOAD)
+        for slot in range(n_slots):
+            load_scale_slot(slot)
+        for lo in range(SLICES_PER_LOAD, N_SLICES, SLICES_PER_LOAD):
+            load_slices(lo, min(lo + SLICES_PER_LOAD, N_SLICES))
+        load_weight(0, 0, K_PASS)
+        load_weight(0, K_PASS, D)
+        for step in range(1, STEPS):
+            load_weight(step, 0, D)
+
+        ident_f32 = keep.tile([P, P], F32)
+        make_identity(nc, ident_f32[:])
+        ident_bf16 = keep.tile([P, P], BF16)
+        make_identity(nc, ident_bf16[:])
+        group_of_row = keep.tile([P, P], F32)
+        nc.vector.memset(group_of_row[:], 0.0)
+        nc.vector.tensor_reduce(
+            out=group_of_row[:, 0:GROUPS],
+            in_=ident_f32[:].rearrange("p (q i) -> p q i", i=ROWS_PER_GROUP),
+            axis=AXIS_X,
+            op=ALU.add,
+        )
+        place_in_group = keep.tile([P, ROWS_PER_GROUP], F32)
+        nc.vector.tensor_reduce(
+            out=place_in_group[:],
+            in_=ident_f32[:].rearrange("p (q i) -> p i q", i=ROWS_PER_GROUP),
+            axis=AXIS_X,
+            op=ALU.add,
+        )
+
+        for slot in range(n_slots):
+            nc.gpsimd.tensor_copy(
+                out=w_planes[:, slot, :].rearrange("p (h t m) -> p h t m", t=PACK, m=P),
+                in_=raw_planes[:, slot, :].rearrange("p (h m t) -> p h t m", t=PACK, m=P),
+            )
+
+        def order_weight(step, h):
+            lo = K_PASS * h
+            nc.vector.tensor_copy(
+                out=w_words[:, step, :, lo : lo + K_PASS].bitcast(I32).rearrange("p g (t m) -> p g t m", t=PACK),
+                in_=raw_words[:, step, :, lo : lo + K_PASS].bitcast(I32).rearrange("p g (m t) -> p g t m", t=PACK),
+            )
+
+        def turn_embedding_slice(n):
+            pairs_of_d = e_raw[:, n, :].bitcast(F32)
+            words_per_pass = K_PASS // 2
+            turned = psum_banks.tile([P, PASSES, 2, P], F32, tag="bank")
+            for g in range(PASSES):
+                for u in range(2):
+                    nc.tensor.transpose(
+                        turned[:, g, u, :],
+                        pairs_of_d[:, words_per_pass * g + u : words_per_pass * (g + 1) : 2],
+                        ident_f32[:],
+                    )
+            grouped = slice_stage.tile([P, PASSES, P, PACK], BF16, tag="grouped", align_bytes=64)
+            nc.scalar.copy(out=grouped[:].bitcast(F32), in_=turned[:].rearrange("p g u b -> p g b u"))
+            return grouped
+
+        def turn_context_slice(n):
+            grouped = slice_stage.tile([P, PASSES, P, PACK], BF16, tag="grouped", align_bytes=64)
+            for g in range(PASSES):
+                turned = psum_banks.tile([P, PACK, P], F32, tag="bank")
+                for t in range(PACK):
+                    lo = K_PASS * g + t
+                    nc.tensor.matmul(
+                        out=turned[:, t, :],
+                        lhsT=c_raw[:, n, lo : K_PASS * (g + 1) : PACK],
+                        rhs=ident_bf16[:],
+                        start=True,
+                        stop=True,
+                    )
+                copy_out = nc.scalar.copy if g == 0 else nc.vector.tensor_copy
+                copy_out(out=grouped[:, g, :, :], in_=turned[:].rearrange("p t j -> p j t"))
+            return grouped
+
+        def quantise(grouped, words, scales):
+            nc.vector.quantize_mx(
+                out=words.rearrange("p g b -> p (g b)").bitcast(FP8X4),
+                scales=scales.rearrange("p g b -> p (g b)"),
+                in_=grouped[:].rearrange("p g b t -> p (g b t)"),
+            )
+
+        staged = {}
+        for n in range(N_SLICES + 1):
+            if n < N_SLICES:
+                staged[n] = (turn_embedding_slice(n), turn_context_slice(n))
+            if n >= 1:
+                grouped_e, grouped_c = staged[n - 1]
+                quantise(grouped_e, e_words[:, n - 1, :, :], e_scales[:, n - 1, :, :])
+                quantise(grouped_c, c_words[:, n - 1, :, :], c_scales[:, n - 1, :, :])
+
+        for h in range(D // K_PASS):
+            order_weight(0, h)
+
+        def project(i):
+            step, s = pairs[i]
+            grouped = xw_stage.tile([P, PASSES, P, PACK], BF16, tag="xw_grouped", align_bytes=64)
+            for g in range(PASSES):
+                bank = psum_banks.tile([P, PACK, P], F32, tag="bank")
+                for t in range(PACK):
+                    lo = K_PASS * g + P * t
+                    for k_pass in range(PASSES):
+                        slot, place = divmod(PASSES * step + k_pass, PLANES_PER_SLOT)
+                        nc.tensor.matmul_mx(
+                            out=bank[:, t, :],
+                            lhsT=w_words[:, step, k_pass, lo : lo + P].bitcast(FP8X4),
+                            lhsT_scale=w_planes[4 * place : P, slot, lo : lo + P],
+                            rhs=e_words[:, step + s, k_pass, :].bitcast(FP8X4),
+                            rhs_scale=e_scales[:, step + s, k_pass, :],
+                            start=(k_pass == 0),
+                            stop=(k_pass == PASSES - 1),
+                        )
+                to_vector = i % 2 == 1 and g == PASSES - 1
+                copy_out = nc.vector.tensor_copy if to_vector else nc.scalar.copy
+                copy_out(out=grouped[:, g, :, :], in_=bank[:].rearrange("p t b -> p b t"))
+            return grouped
+
+        def compare(i):
+            step, s = pairs[i]
+            scores = psum_scores.tile([P, P], F32, tag="scores")
+            for g in range(PASSES):
+                nc.tensor.matmul_mx(
+                    out=scores[:],
+                    lhsT=xw_words[:, i, g, :].bitcast(FP8X4),
+                    lhsT_scale=xw_scales[:, i, g, :],
+                    rhs=c_words[:, s, g, :].bitcast(FP8X4),
+                    rhs_scale=c_scales[:, s, g, :],
+                    start=(g == 0),
+                    stop=(g == PASSES - 1),
+                )
+            nc.vector.tensor_reduce(out=neg_max[:, i : i + 1], in_=scores[:], axis=AXIS_X, op=ALU.max, negate=True)
+            masked = unread.tile([P, P], F32, tag="masked")
+            nc.vector.scalar_tensor_tensor(
+                out=masked[:],
+                in0=scores[:],
+                scalar=1.0,
+                in1=ident_f32[:],
+                op0=ALU.mult,
+                op1=ALU.mult,
+                accum_out=diagonal[:, i : i + 1],
+            )
+            return scores
+
+        def sum_exponentials(i, scores):
+            exponentials = unread.tile([P, P], F32, tag="exponentials")
+            nc.scalar.activation(
+                out=exponentials[:],
+                in_=scores[:],
+                func=ACT.Exp,
+                bias=neg_max[:, i : i + 1],
+                scale=1.0,
+                accum_out=sum_exp[:, i : i + 1],
+            )
+
+        def spread(step, values, spread_tile):
+            n_times = N_SLICES - step
+            lo = first_pair[step]
+            shape = [P, ROWS_PER_GROUP, n_times]
+            nc.vector.tensor_tensor(
+                out=spread_tile[:, ROWS_PER_GROUP * lo : ROWS_PER_GROUP * (lo + n_times)].rearrange(
+                    "p (i s) -> p i s", s=n_times
+                ),
+                in0=values[:, lo : lo + n_times].unsqueeze(1).to_broadcast(shape),
+                in1=place_in_group[:].unsqueeze(2).to_broadcast(shape),
+                op=ALU.mult,
+            )
+
+        def spread_shift_of(step):
+            n_times = N_SLICES - step
+            lo = first_pair[step]
+            nc.vector.scalar_tensor_tensor(
+                out=shift[:, lo : lo + n_times],
+                in0=neg_max[:, lo : lo + n_times],
+                scalar=math.log(P * n_times),
+                in1=diagonal[:, lo : lo + n_times],
+                op0=ALU.add,
+                op1=ALU.add,
+            )
+            spread(step, shift, spread_shift)
+
+        def ends_step(i):
+            step, s = pairs[i]
+            return s == N_SLICES - step - 1
+
+        grouped_of = {}
+        scores_of = {}
+        for i in range(N_PAIRS + EXP_LAG):
+            if 0 <= i - EXP_LAG:
+                sum_exponentials(i - EXP_LAG, scores_of[i - EXP_LAG])
+                if ends_step(i - EXP_LAG):
+                    spread(pairs[i - EXP_LAG][0], sum_exp, spread_sum)
+            if 0 <= i - COMPARE_LAG < N_PAIRS:
+                scores_of[i - COMPARE_LAG] = compare(i - COMPARE_LAG)
+                if ends_step(i - COMPARE_LAG):
+                    spread_shift_of(pairs[i - COMPARE_LAG][0])
+            if 0 <= i - QUANTISE_LAG < N_PAIRS:
+                quantise(
+                    grouped_of[i - QUANTISE_LAG],
+                    xw_words[:, i - QUANTISE_LAG, :, :],
+                    xw_scales[:, i - QUANTISE_LAG, :, :],
+                )
+            for step in range(1, STEPS):
+                for h in range(D // K_PASS):
+                    if i == first_pair[step] - ORDER_LEAD + h:
+                        order_weight(step, h)
+            if i < N_PAIRS:
+                grouped_of[i] = project(i)
+
+        gathered_shift = psum_banks.tile([P, ROWS_PER_GROUP * N_PAIRS], F32, tag="bank")
+        nc.tensor.matmul(out=gathered_shift[:], lhsT=group_of_row[:], rhs=spread_shift[:], start=True, stop=True)
+        gathered_sum = psum_banks.tile([P, ROWS_PER_GROUP * N_PAIRS], F32, tag="bank")
+        nc.tensor.matmul(out=gathered_sum[:], lhsT=group_of_row[:], rhs=spread_sum[:], start=True, stop=True)
+        log_sum = keep.tile([GROUPS, ROWS_PER_GROUP * N_PAIRS], F32)
+        nc.scalar.activation(out=log_sum[:], in_=gathered_sum[0:GROUPS, :], func=ACT.Ln)
+        loss = keep.tile([GROUPS, ROWS_PER_GROUP * N_PAIRS], F32)
+        nc.vector.tensor_tensor(out=loss[:], in0=log_sum[:], in1=gathered_shift[0:GROUPS, :], op=ALU.subtract)
+        for step in range(STEPS):
+            lo = first_pair[step]
+            hi = lo + N_SLICES - step
+            nc.sync.dma_start(
+                out=out[P * lo : P * hi].rearrange("(q r) -> q r", q=GROUPS),
+                in_=loss[:, ROWS_PER_GROUP * lo : ROWS_PER_GROUP * hi],
+            )

@@ -24,13 +24,13 @@ K_PASS = P * PACK
 PASSES = D // K_PASS
 PLANES_PER_SLOT = 4
 QUADRANT = 32
-SLICES_PER_LOAD = 2
+SLICES_AHEAD = 2
+W_PARTS = 4
 ROWS_PER_GROUP = 8
 GROUPS = P // ROWS_PER_GROUP
 QUANTISE_LAG = 1
 COMPARE_LAG = 3
 EXP_LAG = 4
-ORDER_LEAD = 4
 
 N_PAIRS = sum(N_SLICES - step for step in range(STEPS))
 FLOPS = 2 * N_PAIRS * P * D * D + 2 * N_PAIRS * P * P * D
@@ -71,11 +71,14 @@ def tile_infonceloss_pa_e_kernel(tc, embeddings, contexts, W_words, W_scales, ou
         spread_sum = keep.tile([P, ROWS_PER_GROUP * N_PAIRS], F32)
         spread_shift = keep.tile([P, ROWS_PER_GROUP * N_PAIRS], F32)
 
-        nc.vector.memset(raw_planes[:].bitcast(I32), 0)
+        def load_slice(source, raw, n, first_time):
+            nc.sync.dma_start(out=raw[:, n, :], in_=source[:, first_time + n, :])
 
-        def load_slices(lo, hi):
-            nc.sync.dma_start(out=e_raw[:, lo:hi, :], in_=embeddings[:, 1 + lo : 1 + hi, :])
-            nc.sync.dma_start(out=c_raw[:, lo:hi, :], in_=contexts[:, lo:hi, :])
+        def load_e(n):
+            load_slice(embeddings, e_raw, n, 1)
+
+        def load_c(n):
+            load_slice(contexts, c_raw, n, 0)
 
         def load_scale_slot(slot):
             lo = PLANES_PER_SLOT * slot
@@ -95,79 +98,71 @@ def tile_infonceloss_pa_e_kernel(tc, embeddings, contexts, W_words, W_scales, ou
                 .bitcast(I32),
             )
 
-        load_slices(0, SLICES_PER_LOAD)
-        for slot in range(n_slots):
-            load_scale_slot(slot)
-        for lo in range(SLICES_PER_LOAD, N_SLICES, SLICES_PER_LOAD):
-            load_slices(lo, min(lo + SLICES_PER_LOAD, N_SLICES))
+        nc.vector.memset(raw_planes[:, 0, :].bitcast(I32), 0)
+        nc.vector.memset(raw_planes[:, 1:n_slots, :].bitcast(I32), 0)
+
+        load_scale_slot(0)
+        for n in range(SLICES_AHEAD):
+            load_e(n)
         load_weight(0, 0, K_PASS)
         load_weight(0, K_PASS, D)
-        for step in range(1, STEPS):
+        for n in range(SLICES_AHEAD, N_SLICES):
+            load_e(n)
+            load_c(n - SLICES_AHEAD)
+        load_weight(1, 0, D)
+        for n in range(N_SLICES - SLICES_AHEAD, N_SLICES):
+            load_c(n)
+        load_weight(2, 0, D)
+        for slot in range(1, n_slots):
+            load_scale_slot(slot)
+        for step in range(3, STEPS):
             load_weight(step, 0, D)
 
-        ident_f32 = keep.tile([P, P], F32)
-        make_identity(nc, ident_f32[:])
-        ident_bf16 = keep.tile([P, P], BF16)
-        make_identity(nc, ident_bf16[:])
+        ident = keep.tile([P, P], F32)
+        make_identity(nc, ident[:])
         group_of_row = keep.tile([P, P], F32)
         nc.vector.memset(group_of_row[:], 0.0)
         nc.vector.tensor_reduce(
             out=group_of_row[:, 0:GROUPS],
-            in_=ident_f32[:].rearrange("p (q i) -> p q i", i=ROWS_PER_GROUP),
+            in_=ident[:].rearrange("p (q i) -> p q i", i=ROWS_PER_GROUP),
             axis=AXIS_X,
             op=ALU.add,
         )
         place_in_group = keep.tile([P, ROWS_PER_GROUP], F32)
         nc.vector.tensor_reduce(
             out=place_in_group[:],
-            in_=ident_f32[:].rearrange("p (q i) -> p i q", i=ROWS_PER_GROUP),
+            in_=ident[:].rearrange("p (q i) -> p i q", i=ROWS_PER_GROUP),
             axis=AXIS_X,
             op=ALU.add,
         )
 
-        for slot in range(n_slots):
-            nc.gpsimd.tensor_copy(
+        def order_scales(slot, copy):
+            copy(
                 out=w_planes[:, slot, :].rearrange("p (h t m) -> p h t m", t=PACK, m=P),
                 in_=raw_planes[:, slot, :].rearrange("p (h m t) -> p h t m", t=PACK, m=P),
             )
 
-        def order_weight(step, h):
-            lo = K_PASS * h
+        def order_weight(step, part):
+            h, g = divmod(part, PASSES)
+            cols = slice(K_PASS * h, K_PASS * (h + 1))
             nc.vector.tensor_copy(
-                out=w_words[:, step, :, lo : lo + K_PASS].bitcast(I32).rearrange("p g (t m) -> p g t m", t=PACK),
-                in_=raw_words[:, step, :, lo : lo + K_PASS].bitcast(I32).rearrange("p g (m t) -> p g t m", t=PACK),
+                out=w_words[:, step, g, cols].bitcast(I32).rearrange("p (t m) -> p t m", t=PACK),
+                in_=raw_words[:, step, g, cols].bitcast(I32).rearrange("p (m t) -> p t m", t=PACK),
             )
 
-        def turn_embedding_slice(n):
-            pairs_of_d = e_raw[:, n, :].bitcast(F32)
+        def turn_slice(raw, n, copy):
+            pairs_of_values = raw[:, n, :].bitcast(F32)
             words_per_pass = K_PASS // 2
             turned = psum_banks.tile([P, PASSES, 2, P], F32, tag="bank")
             for g in range(PASSES):
                 for u in range(2):
                     nc.tensor.transpose(
                         turned[:, g, u, :],
-                        pairs_of_d[:, words_per_pass * g + u : words_per_pass * (g + 1) : 2],
-                        ident_f32[:],
+                        pairs_of_values[:, words_per_pass * g + u : words_per_pass * (g + 1) : 2],
+                        ident[:],
                     )
             grouped = slice_stage.tile([P, PASSES, P, PACK], BF16, tag="grouped", align_bytes=64)
-            nc.scalar.copy(out=grouped[:].bitcast(F32), in_=turned[:].rearrange("p g u b -> p g b u"))
-            return grouped
-
-        def turn_context_slice(n):
-            grouped = slice_stage.tile([P, PASSES, P, PACK], BF16, tag="grouped", align_bytes=64)
-            for g in range(PASSES):
-                turned = psum_banks.tile([P, PACK, P], F32, tag="bank")
-                for t in range(PACK):
-                    lo = K_PASS * g + t
-                    nc.tensor.matmul(
-                        out=turned[:, t, :],
-                        lhsT=c_raw[:, n, lo : K_PASS * (g + 1) : PACK],
-                        rhs=ident_bf16[:],
-                        start=True,
-                        stop=True,
-                    )
-                copy_out = nc.scalar.copy if g == 0 else nc.vector.tensor_copy
-                copy_out(out=grouped[:, g, :, :], in_=turned[:].rearrange("p t j -> p j t"))
+            copy(out=grouped[:].bitcast(F32), in_=turned[:].rearrange("p g u b -> p g b u"))
             return grouped
 
         def quantise(grouped, words, scales):
@@ -177,17 +172,20 @@ def tile_infonceloss_pa_e_kernel(tc, embeddings, contexts, W_words, W_scales, ou
                 in_=grouped[:].rearrange("p g b t -> p (g b t)"),
             )
 
-        staged = {}
-        for n in range(N_SLICES + 1):
-            if n < N_SLICES:
-                staged[n] = (turn_embedding_slice(n), turn_context_slice(n))
-            if n >= 1:
-                grouped_e, grouped_c = staged[n - 1]
-                quantise(grouped_e, e_words[:, n - 1, :, :], e_scales[:, n - 1, :, :])
-                quantise(grouped_c, c_words[:, n - 1, :, :], c_scales[:, n - 1, :, :])
+        def quantise_e(n, grouped):
+            quantise(grouped, e_words[:, n, :, :], e_scales[:, n, :, :])
 
-        for h in range(D // K_PASS):
-            order_weight(0, h)
+        def quantise_c(n, grouped):
+            quantise(grouped, c_words[:, n, :, :], c_scales[:, n, :, :])
+
+        order_scales(0, nc.vector.tensor_copy)
+        for slot in range(1, n_slots):
+            order_scales(slot, nc.gpsimd.tensor_copy)
+        early = [turn_slice(e_raw, n, nc.scalar.copy) for n in range(SLICES_AHEAD)]
+        for n in range(SLICES_AHEAD):
+            quantise_e(n, early[n])
+        for part in range(W_PARTS):
+            order_weight(0, part)
 
         def project(i):
             step, s = pairs[i]
@@ -207,7 +205,7 @@ def tile_infonceloss_pa_e_kernel(tc, embeddings, contexts, W_words, W_scales, ou
                             start=(k_pass == 0),
                             stop=(k_pass == PASSES - 1),
                         )
-                to_vector = i % 2 == 1 and g == PASSES - 1
+                to_vector = step > 0 and i % 2 == 1 and g == PASSES - 1
                 copy_out = nc.vector.tensor_copy if to_vector else nc.scalar.copy
                 copy_out(out=grouped[:, g, :, :], in_=bank[:].rearrange("p t b -> p b t"))
             return grouped
@@ -231,7 +229,7 @@ def tile_infonceloss_pa_e_kernel(tc, embeddings, contexts, W_words, W_scales, ou
                 out=masked[:],
                 in0=scores[:],
                 scalar=1.0,
-                in1=ident_f32[:],
+                in1=ident[:],
                 op0=ALU.mult,
                 op1=ALU.mult,
                 accum_out=diagonal[:, i : i + 1],
@@ -281,6 +279,8 @@ def tile_infonceloss_pa_e_kernel(tc, embeddings, contexts, W_words, W_scales, ou
 
         grouped_of = {}
         scores_of = {}
+        turned_e = {}
+        turned_c = {}
         for i in range(N_PAIRS + EXP_LAG):
             if 0 <= i - EXP_LAG:
                 sum_exponentials(i - EXP_LAG, scores_of[i - EXP_LAG])
@@ -296,12 +296,19 @@ def tile_infonceloss_pa_e_kernel(tc, embeddings, contexts, W_words, W_scales, ou
                     xw_words[:, i - QUANTISE_LAG, :, :],
                     xw_scales[:, i - QUANTISE_LAG, :, :],
                 )
+            if i - 1 in turned_e:
+                quantise_e(i - 1 + SLICES_AHEAD, turned_e[i - 1])
+            if i - 1 in turned_c:
+                quantise_c(i - 1, turned_c[i - 1])
             for step in range(1, STEPS):
-                for h in range(D // K_PASS):
-                    if i == first_pair[step] - ORDER_LEAD + h:
-                        order_weight(step, h)
+                if 0 <= i - (first_pair[step] - W_PARTS) < W_PARTS:
+                    order_weight(step, i - (first_pair[step] - W_PARTS))
             if i < N_PAIRS:
                 grouped_of[i] = project(i)
+            if i + SLICES_AHEAD < N_SLICES:
+                turned_e[i] = turn_slice(e_raw, i + SLICES_AHEAD, nc.scalar.copy)
+            if i < N_SLICES:
+                turned_c[i] = turn_slice(c_raw, i, nc.vector.tensor_copy)
 
         gathered_shift = psum_banks.tile([P, ROWS_PER_GROUP * N_PAIRS], F32, tag="bank")
         nc.tensor.matmul(out=gathered_shift[:], lhsT=group_of_row[:], rhs=spread_shift[:], start=True, stop=True)

@@ -146,8 +146,8 @@ def tile_infonceloss_pa_e_kernel(tc, embeddings, contexts, W_words, W_scales, ou
             h, g = divmod(part, PASSES)
             cols = slice(K_PASS * h, K_PASS * (h + 1))
             nc.vector.tensor_copy(
-                out=w_words[:, step, g, cols].bitcast(I32).rearrange("p (t m) -> p t m", t=PACK),
-                in_=raw_words[:, step, g, cols].bitcast(I32).rearrange("p (m t) -> p t m", t=PACK),
+                out=w_words[:, step, g, cols].bitcast(I32).rearrange("p (t m i) -> p m t i", t=PACK, i=PACK),
+                in_=raw_words[:, step, g, cols].bitcast(I32).rearrange("p (m i t) -> p m t i", t=PACK, i=PACK),
             )
 
         def turn_slice(raw, n, copy):

@@ -24,13 +24,21 @@ K_PASS = P * PACK
 PASSES = D // K_PASS
 PLANES_PER_SLOT = 4
 QUADRANT = 32
-SLICES_AHEAD = 2
+SLICES_AHEAD = 4
+TURNS = (
+    (("e", 4), ("c", 0)),
+    (("e", 5), ("c", 1)),
+    (("e", 6), ("c", 2)),
+    (("c", 3),),
+    (("c", 4),),
+    (("c", 5),),
+    (("c", 6),),
+)
 W_PARTS = 4
 ROWS_PER_GROUP = 8
 GROUPS = P // ROWS_PER_GROUP
 QUANTISE_LAG = 1
 COMPARE_LAG = 3
-EXP_LAG = 4
 
 N_PAIRS = sum(N_SLICES - step for step in range(STEPS))
 FLOPS = 2 * N_PAIRS * P * D * D + 2 * N_PAIRS * P * P * D
@@ -106,12 +114,11 @@ def tile_infonceloss_pa_e_kernel(tc, embeddings, contexts, W_words, W_scales, ou
             load_e(n)
         load_weight(0, 0, K_PASS)
         load_weight(0, K_PASS, D)
-        for n in range(SLICES_AHEAD, N_SLICES):
-            load_e(n)
-            load_c(n - SLICES_AHEAD)
-        load_weight(1, 0, D)
-        for n in range(N_SLICES - SLICES_AHEAD, N_SLICES):
-            load_c(n)
+        for i, turns in enumerate(TURNS):
+            if i == first_pair[1] - W_PARTS + 1:
+                load_weight(1, 0, D)
+            for kind, n in turns:
+                (load_e if kind == "e" else load_c)(n)
         load_weight(2, 0, D)
         for slot in range(1, n_slots):
             load_scale_slot(slot)
@@ -212,7 +219,8 @@ def tile_infonceloss_pa_e_kernel(tc, embeddings, contexts, W_words, W_scales, ou
 
         def compare(i):
             step, s = pairs[i]
-            scores = psum_scores.tile([P, P], F32, tag="scores")
+            pool, tag = (psum_scores, "scores") if i < N_PAIRS - 2 else (psum_banks, "bank")
+            scores = pool.tile([P, P], F32, tag=tag)
             for g in range(PASSES):
                 nc.tensor.matmul_mx(
                     out=scores[:],
@@ -273,51 +281,77 @@ def tile_infonceloss_pa_e_kernel(tc, embeddings, contexts, W_words, W_scales, ou
             )
             spread(step, shift, spread_shift)
 
+        gathered = {}
+
+        def gather(steps):
+            if not gathered:
+                for name in ("shift", "sum"):
+                    bank = psum_banks.tile([P, ROWS_PER_GROUP * N_PAIRS], F32, tag="bank")
+                    gathered[name] = bank
+            lo = ROWS_PER_GROUP * first_pair[steps[0]]
+            hi = ROWS_PER_GROUP * (first_pair[steps[-1]] + N_SLICES - steps[-1])
+            for name, values in (("shift", spread_shift), ("sum", spread_sum)):
+                nc.tensor.matmul(
+                    out=gathered[name][:, lo:hi], lhsT=group_of_row[:], rhs=values[:, lo:hi], start=True, stop=True
+                )
+
         def ends_step(i):
             step, s = pairs[i]
             return s == N_SLICES - step - 1
 
+        last = N_PAIRS - 1
+
+        def compare_round(n):
+            return min(n + COMPARE_LAG, max(n + COMPARE_LAG - 1, last))
+
         grouped_of = {}
         scores_of = {}
-        turned_e = {}
-        turned_c = {}
-        for i in range(N_PAIRS + EXP_LAG):
-            if 0 <= i - EXP_LAG:
-                sum_exponentials(i - EXP_LAG, scores_of[i - EXP_LAG])
-                if ends_step(i - EXP_LAG):
-                    spread(pairs[i - EXP_LAG][0], sum_exp, spread_sum)
-            if 0 <= i - COMPARE_LAG < N_PAIRS:
-                scores_of[i - COMPARE_LAG] = compare(i - COMPARE_LAG)
-                if ends_step(i - COMPARE_LAG):
-                    spread_shift_of(pairs[i - COMPARE_LAG][0])
-            if 0 <= i - QUANTISE_LAG < N_PAIRS:
+        turned = {}
+        for i in range(compare_round(last) + 2):
+            summed = [n for n in range(N_PAIRS) if compare_round(n) + 1 == i]
+            for n in summed:
+                sum_exponentials(n, scores_of[n])
+            for n in range(N_PAIRS):
+                if compare_round(n) == i:
+                    scores_of[n] = compare(n)
+                    if ends_step(n):
+                        spread_shift_of(pairs[n][0])
+            if 0 <= i - QUANTISE_LAG < last:
                 quantise(
                     grouped_of[i - QUANTISE_LAG],
                     xw_words[:, i - QUANTISE_LAG, :, :],
                     xw_scales[:, i - QUANTISE_LAG, :, :],
                 )
-            if i - 1 in turned_e:
-                quantise_e(i - 1 + SLICES_AHEAD, turned_e[i - 1])
-            if i - 1 in turned_c:
-                quantise_c(i - 1, turned_c[i - 1])
+            for n in summed:
+                if ends_step(n):
+                    spread(pairs[n][0], sum_exp, spread_sum)
+            if 0 < i <= len(TURNS):
+                for kind, n in TURNS[i - 1]:
+                    (quantise_e if kind == "e" else quantise_c)(n, turned[kind, n])
             for step in range(1, STEPS):
                 if 0 <= i - (first_pair[step] - W_PARTS) < W_PARTS:
                     order_weight(step, i - (first_pair[step] - W_PARTS))
             if i < N_PAIRS:
                 grouped_of[i] = project(i)
-            if i + SLICES_AHEAD < N_SLICES:
-                turned_e[i] = turn_slice(e_raw, i + SLICES_AHEAD, nc.scalar.copy)
-            if i < N_SLICES:
-                turned_c[i] = turn_slice(c_raw, i, nc.vector.tensor_copy)
+            if i == last:
+                for g in range(PASSES):
+                    nc.vector.quantize_mx(
+                        out=xw_words[:, i, g, :].bitcast(FP8X4),
+                        scales=xw_scales[:, i, g, :],
+                        in_=grouped_of[i][:, g, :, :].rearrange("p b t -> p (b t)"),
+                    )
+            if i < len(TURNS):
+                for place, (kind, n) in enumerate(TURNS[i]):
+                    copy_out = nc.vector.tensor_copy if place == 1 else nc.scalar.copy
+                    turned[kind, n] = turn_slice(e_raw if kind == "e" else c_raw, n, copy_out)
+            if i == compare_round(last):
+                gather(range(STEPS - 1))
 
-        gathered_shift = psum_banks.tile([P, ROWS_PER_GROUP * N_PAIRS], F32, tag="bank")
-        nc.tensor.matmul(out=gathered_shift[:], lhsT=group_of_row[:], rhs=spread_shift[:], start=True, stop=True)
-        gathered_sum = psum_banks.tile([P, ROWS_PER_GROUP * N_PAIRS], F32, tag="bank")
-        nc.tensor.matmul(out=gathered_sum[:], lhsT=group_of_row[:], rhs=spread_sum[:], start=True, stop=True)
+        gather(range(STEPS - 1, STEPS))
         log_sum = keep.tile([GROUPS, ROWS_PER_GROUP * N_PAIRS], F32)
-        nc.scalar.activation(out=log_sum[:], in_=gathered_sum[0:GROUPS, :], func=ACT.Ln)
+        nc.scalar.activation(out=log_sum[:], in_=gathered["sum"][0:GROUPS, :], func=ACT.Ln)
         loss = keep.tile([GROUPS, ROWS_PER_GROUP * N_PAIRS], F32)
-        nc.vector.tensor_tensor(out=loss[:], in0=log_sum[:], in1=gathered_shift[0:GROUPS, :], op=ALU.subtract)
+        nc.vector.tensor_tensor(out=loss[:], in0=log_sum[:], in1=gathered["shift"][0:GROUPS, :], op=ALU.subtract)
         for step in range(STEPS):
             lo = first_pair[step]
             hi = lo + N_SLICES - step

@@ -34,6 +34,10 @@ TURNS = (
     (("c", 5),),
     (("c", 6),),
 )
+WARM_COLS = 512
+WARM_BEFORE = 7
+WARM_BETWEEN = 1
+WARM_AFTER = 2
 W_PARTS = 4
 ROWS_PER_GROUP = 8
 GROUPS = P // ROWS_PER_GROUP
@@ -105,6 +109,14 @@ def tile_infonceloss_pa_e_kernel(tc, embeddings, contexts, W_words, W_scales, ou
                 .rearrange("g p n t -> p g (n t)")[:, :, PACK * lo : PACK * hi]
                 .bitcast(I32),
             )
+
+        zeros = keep.tile([P, WARM_COLS], BF16)
+        nc.vector.memset(zeros[:], 0.0)
+        warm_bank = psum_scores.tile([P, WARM_COLS], F32, tag="scores")
+
+        def keep_warm(times):
+            for turn in range(times):
+                nc.tensor.matmul(out=warm_bank[:], lhsT=zeros[:, 0:P], rhs=zeros[:], start=True, stop=True)
 
         nc.vector.memset(raw_planes[:, 0, :].bitcast(I32), 0)
         nc.vector.memset(raw_planes[:, 1:n_slots, :].bitcast(I32), 0)
@@ -188,7 +200,12 @@ def tile_infonceloss_pa_e_kernel(tc, embeddings, contexts, W_words, W_scales, ou
         order_scales(0, nc.vector.tensor_copy)
         for slot in range(1, n_slots):
             order_scales(slot, nc.gpsimd.tensor_copy)
-        early = [turn_slice(e_raw, n, nc.scalar.copy) for n in range(SLICES_AHEAD)]
+        keep_warm(WARM_BEFORE)
+        early = []
+        for n in range(SLICES_AHEAD):
+            early.append(turn_slice(e_raw, n, nc.scalar.copy))
+            keep_warm(WARM_BETWEEN)
+        keep_warm(WARM_AFTER)
         for n in range(SLICES_AHEAD):
             quantise_e(n, early[n])
         for part in range(W_PARTS):

@@ -111,7 +111,7 @@ def tile_infonceloss_pa_e_kernel(tc, embeddings, contexts, W_words, W_scales, ou
             )
 
         zeros = keep.tile([P, WARM_COLS], BF16)
-        nc.vector.memset(zeros[:], 0.0)
+        nc.vector.memset(zeros[:].bitcast(I32), 0)
         warm_bank = psum_scores.tile([P, WARM_COLS], F32, tag="scores")
 
         def keep_warm(times):
@@ -121,8 +121,9 @@ def tile_infonceloss_pa_e_kernel(tc, embeddings, contexts, W_words, W_scales, ou
         nc.vector.memset(raw_planes[:, 0, :].bitcast(I32), 0)
         nc.vector.memset(raw_planes[:, 1:n_slots, :].bitcast(I32), 0)
 
+        load_e(0)
         load_scale_slot(0)
-        for n in range(SLICES_AHEAD):
+        for n in range(1, SLICES_AHEAD):
             load_e(n)
         load_weight(0, 0, K_PASS)
         load_weight(0, K_PASS, D)
@@ -169,17 +170,24 @@ def tile_infonceloss_pa_e_kernel(tc, embeddings, contexts, W_words, W_scales, ou
                 in_=raw_words[:, step, g, cols].bitcast(I32).rearrange("p (m i t) -> p m t i", t=PACK, i=PACK),
             )
 
-        def turn_slice(raw, n, copy):
+        def part_words(raw, n):
+            parted = slice_stage.tile([P, PASSES, 2, P], I32, tag="parted", bufs=10)
+            nc.gpsimd.tensor_copy(
+                out=parted[:], in_=raw[:, n, :].bitcast(I32).rearrange("b (g p u) -> b g u p", g=PASSES, u=2)
+            )
+            return parted
+
+        def turn_slice(raw, n, copy, parted=None):
             pairs_of_values = raw[:, n, :].bitcast(F32)
             words_per_pass = K_PASS // 2
             turned = psum_banks.tile([P, PASSES, 2, P], F32, tag="bank")
             for g in range(PASSES):
                 for u in range(2):
-                    nc.tensor.transpose(
-                        turned[:, g, u, :],
-                        pairs_of_values[:, words_per_pass * g + u : words_per_pass * (g + 1) : 2],
-                        ident[:],
-                    )
+                    if parted is None:
+                        words = pairs_of_values[:, words_per_pass * g + u : words_per_pass * (g + 1) : 2]
+                    else:
+                        words = parted[:, g, u, :].bitcast(F32)
+                    nc.tensor.transpose(turned[:, g, u, :], words, ident[:])
             grouped = slice_stage.tile([P, PASSES, P, PACK], BF16, tag="grouped", align_bytes=64)
             copy(out=grouped[:].bitcast(F32), in_=turned[:].rearrange("p g u b -> p g b u"))
             return grouped
@@ -198,6 +206,10 @@ def tile_infonceloss_pa_e_kernel(tc, embeddings, contexts, W_words, W_scales, ou
             quantise(grouped, c_words[:, n, :, :], c_scales[:, n, :, :])
 
         order_scales(0, nc.vector.tensor_copy)
+        parted = {}
+        for turns in TURNS:
+            for kind, n in turns:
+                parted[kind, n] = part_words(e_raw if kind == "e" else c_raw, n)
         for slot in range(1, n_slots):
             order_scales(slot, nc.gpsimd.tensor_copy)
         keep_warm(WARM_BEFORE)
@@ -208,8 +220,9 @@ def tile_infonceloss_pa_e_kernel(tc, embeddings, contexts, W_words, W_scales, ou
         keep_warm(WARM_AFTER)
         for n in range(SLICES_AHEAD):
             quantise_e(n, early[n])
-        for part in range(W_PARTS):
-            order_weight(0, part)
+            if n % 2 == 1:
+                for part in range(PASSES):
+                    order_weight(0, PASSES * (n // 2) + part)
 
         def project(i):
             step, s = pairs[i]
@@ -360,7 +373,7 @@ def tile_infonceloss_pa_e_kernel(tc, embeddings, contexts, W_words, W_scales, ou
             if i < len(TURNS):
                 for place, (kind, n) in enumerate(TURNS[i]):
                     copy_out = nc.vector.tensor_copy if place == 1 else nc.scalar.copy
-                    turned[kind, n] = turn_slice(e_raw if kind == "e" else c_raw, n, copy_out)
+                    turned[kind, n] = turn_slice(e_raw if kind == "e" else c_raw, n, copy_out, parted[kind, n])
             if i == compare_round(last):
                 gather(range(STEPS - 1))
 

@@ -29,10 +29,9 @@ TURNS = (
     (("e", 4), ("c", 0)),
     (("e", 5), ("c", 1)),
     (("e", 6), ("c", 2)),
-    (("c", 3),),
-    (("c", 4),),
-    (("c", 5),),
-    (("c", 6),),
+    (("c", 3), ("c", 4)),
+    (),
+    (("c", 5), ("c", 6)),
 )
 WARM_COLS = 512
 WARM_BEFORE = 7
@@ -43,6 +42,7 @@ ROWS_PER_GROUP = 8
 GROUPS = P // ROWS_PER_GROUP
 QUANTISE_LAG = 1
 COMPARE_LAG = 3
+EXP_LAG = 4
 
 N_PAIRS = sum(N_SLICES - step for step in range(STEPS))
 FLOPS = 2 * N_PAIRS * P * D * D + 2 * N_PAIRS * P * P * D
@@ -58,8 +58,8 @@ def tile_infonceloss_pa_e_kernel(tc, embeddings, contexts, W_words, W_scales, ou
         slice_stage = ctx.enter_context(tc.tile_pool(name="slice_stage", bufs=4))
         xw_stage = ctx.enter_context(tc.tile_pool(name="xw_stage", bufs=3))
         unread = ctx.enter_context(tc.tile_pool(name="unread", bufs=4))
-        psum_banks = ctx.enter_context(tc.psum_pool(name="psum_banks", bufs=6))
-        psum_scores = ctx.enter_context(tc.psum_pool(name="psum_scores", bufs=2))
+        psum_banks = ctx.enter_context(tc.psum_pool(name="psum_banks", bufs=5))
+        psum_scores = ctx.enter_context(tc.psum_pool(name="psum_scores", bufs=3))
         ctx.enter_context(tc.manual_schedule())
 
         e_raw = keep.tile([P, N_SLICES, D], BF16)
@@ -156,11 +156,15 @@ def tile_infonceloss_pa_e_kernel(tc, embeddings, contexts, W_words, W_scales, ou
             op=ALU.add,
         )
 
-        def order_scales(slot, copy):
-            copy(
-                out=w_planes[:, slot, :].rearrange("p (h t m) -> p h t m", t=PACK, m=P),
-                in_=raw_planes[:, slot, :].rearrange("p (h m t) -> p h t m", t=PACK, m=P),
-            )
+        def order_scales(slot, copy, pieces):
+            for h in range(D // K_PASS):
+                cols = slice(K_PASS * h, K_PASS * (h + 1))
+                for piece in range(pieces):
+                    ts = slice(PACK // pieces * piece, PACK // pieces * (piece + 1))
+                    copy(
+                        out=w_planes[:, slot, cols].rearrange("p (t m) -> p t m", t=PACK)[:, ts, :],
+                        in_=raw_planes[:, slot, cols].rearrange("p (m t) -> p t m", t=PACK)[:, ts, :],
+                    )
 
         def order_weight(step, part):
             h, g = divmod(part, PASSES)
@@ -172,9 +176,9 @@ def tile_infonceloss_pa_e_kernel(tc, embeddings, contexts, W_words, W_scales, ou
 
         def part_words(raw, n):
             parted = slice_stage.tile([P, PASSES, 2, P], I32, tag="parted", bufs=10)
-            nc.gpsimd.tensor_copy(
-                out=parted[:], in_=raw[:, n, :].bitcast(I32).rearrange("b (g p u) -> b g u p", g=PASSES, u=2)
-            )
+            words = raw[:, n, :].bitcast(I32).rearrange("b (g p u) -> b g u p", g=PASSES, u=2)
+            for g in range(PASSES):
+                nc.gpsimd.tensor_copy(out=parted[:, g, :, :], in_=words[:, g, :, :])
             return parted
 
         def turn_slice(raw, n, copy, parted=None):
@@ -205,13 +209,12 @@ def tile_infonceloss_pa_e_kernel(tc, embeddings, contexts, W_words, W_scales, ou
         def quantise_c(n, grouped):
             quantise(grouped, c_words[:, n, :, :], c_scales[:, n, :, :])
 
-        order_scales(0, nc.vector.tensor_copy)
         parted = {}
         for turns in TURNS:
             for kind, n in turns:
                 parted[kind, n] = part_words(e_raw if kind == "e" else c_raw, n)
         for slot in range(1, n_slots):
-            order_scales(slot, nc.gpsimd.tensor_copy)
+            order_scales(slot, nc.gpsimd.tensor_copy, 2)
         keep_warm(WARM_BEFORE)
         early = []
         for n in range(SLICES_AHEAD):
@@ -220,6 +223,8 @@ def tile_infonceloss_pa_e_kernel(tc, embeddings, contexts, W_words, W_scales, ou
         keep_warm(WARM_AFTER)
         for n in range(SLICES_AHEAD):
             quantise_e(n, early[n])
+            if n == 0:
+                order_scales(0, nc.vector.tensor_copy, 1)
             if n % 2 == 1:
                 for part in range(PASSES):
                     order_weight(0, PASSES * (n // 2) + part)
@@ -242,7 +247,7 @@ def tile_infonceloss_pa_e_kernel(tc, embeddings, contexts, W_words, W_scales, ou
                             start=(k_pass == 0),
                             stop=(k_pass == PASSES - 1),
                         )
-                to_vector = step > 0 and i % 2 == 1 and g == PASSES - 1
+                to_vector = step > 0 and i % 2 == 1 and i < N_PAIRS - 2 and g == PASSES - 1
                 copy_out = nc.vector.tensor_copy if to_vector else nc.scalar.copy
                 copy_out(out=grouped[:, g, :, :], in_=bank[:].rearrange("p t b -> p b t"))
             return grouped
@@ -262,6 +267,9 @@ def tile_infonceloss_pa_e_kernel(tc, embeddings, contexts, W_words, W_scales, ou
                     stop=(g == PASSES - 1),
                 )
             nc.vector.tensor_reduce(out=neg_max[:, i : i + 1], in_=scores[:], axis=AXIS_X, op=ALU.max, negate=True)
+            return scores
+
+        def take_diagonal(i, scores):
             masked = unread.tile([P, P], F32, tag="masked")
             nc.vector.scalar_tensor_tensor(
                 out=masked[:],
@@ -272,7 +280,6 @@ def tile_infonceloss_pa_e_kernel(tc, embeddings, contexts, W_words, W_scales, ou
                 op1=ALU.mult,
                 accum_out=diagonal[:, i : i + 1],
             )
-            return scores
 
         def sum_exponentials(i, scores):
             exponentials = unread.tile([P, P], F32, tag="exponentials")
@@ -320,7 +327,7 @@ def tile_infonceloss_pa_e_kernel(tc, embeddings, contexts, W_words, W_scales, ou
                     gathered[name] = bank
             lo = ROWS_PER_GROUP * first_pair[steps[0]]
             hi = ROWS_PER_GROUP * (first_pair[steps[-1]] + N_SLICES - steps[-1])
-            for name, values in (("shift", spread_shift), ("sum", spread_sum)):
+            for name, values in (("sum", spread_sum), ("shift", spread_shift)):
                 nc.tensor.matmul(
                     out=gathered[name][:, lo:hi], lhsT=group_of_row[:], rhs=values[:, lo:hi], start=True, stop=True
                 )
@@ -330,54 +337,68 @@ def tile_infonceloss_pa_e_kernel(tc, embeddings, contexts, W_words, W_scales, ou
             return s == N_SLICES - step - 1
 
         last = N_PAIRS - 1
-
-        def compare_round(n):
-            return min(n + COMPARE_LAG, max(n + COMPARE_LAG - 1, last))
-
         grouped_of = {}
         scores_of = {}
         turned = {}
-        for i in range(compare_round(last) + 2):
-            summed = [n for n in range(N_PAIRS) if compare_round(n) + 1 == i]
-            for n in summed:
-                sum_exponentials(n, scores_of[n])
-            for n in range(N_PAIRS):
-                if compare_round(n) == i:
-                    scores_of[n] = compare(n)
-                    if ends_step(n):
-                        spread_shift_of(pairs[n][0])
-            if 0 <= i - QUANTISE_LAG < last:
-                quantise(
-                    grouped_of[i - QUANTISE_LAG],
-                    xw_words[:, i - QUANTISE_LAG, :, :],
-                    xw_scales[:, i - QUANTISE_LAG, :, :],
-                )
-            for n in summed:
-                if ends_step(n):
-                    spread(pairs[n][0], sum_exp, spread_sum)
+
+        def finish_scores(n):
+            take_diagonal(n, scores_of[n])
+            if ends_step(n):
+                spread_shift_of(pairs[n][0])
+
+        def quantise_pair(n):
+            quantise(grouped_of[n], xw_words[:, n, :, :], xw_scales[:, n, :, :])
+
+        for i in range(N_PAIRS):
+            if 0 <= i - EXP_LAG:
+                sum_exponentials(i - EXP_LAG, scores_of[i - EXP_LAG])
+            if 0 <= i - COMPARE_LAG:
+                scores_of[i - COMPARE_LAG] = compare(i - COMPARE_LAG)
+                if i < last:
+                    finish_scores(i - COMPARE_LAG)
+            if i == last:
+                scores_of[last - 2] = compare(last - 2)
+                for n in (last - COMPARE_LAG, last - 2):
+                    sum_exponentials(n, scores_of[n])
+            if i >= 1:
+                quantise_pair(i - 1)
+            if 0 <= i - EXP_LAG and ends_step(i - EXP_LAG):
+                spread(pairs[i - EXP_LAG][0], sum_exp, spread_sum)
             if 0 < i <= len(TURNS):
                 for kind, n in TURNS[i - 1]:
                     (quantise_e if kind == "e" else quantise_c)(n, turned[kind, n])
             for step in range(1, STEPS):
                 if 0 <= i - (first_pair[step] - W_PARTS) < W_PARTS:
                     order_weight(step, i - (first_pair[step] - W_PARTS))
-            if i < N_PAIRS:
-                grouped_of[i] = project(i)
             if i == last:
-                for g in range(PASSES):
-                    nc.vector.quantize_mx(
-                        out=xw_words[:, i, g, :].bitcast(FP8X4),
-                        scales=xw_scales[:, i, g, :],
-                        in_=grouped_of[i][:, g, :, :].rearrange("p b t -> p (b t)"),
-                    )
+                for n in (last - COMPARE_LAG, last - 2):
+                    finish_scores(n)
+                spread(STEPS - 2, sum_exp, spread_sum)
+            grouped_of[i] = project(i)
             if i < len(TURNS):
                 for place, (kind, n) in enumerate(TURNS[i]):
                     copy_out = nc.vector.tensor_copy if place == 1 else nc.scalar.copy
                     turned[kind, n] = turn_slice(e_raw if kind == "e" else c_raw, n, copy_out, parted[kind, n])
-            if i == compare_round(last):
-                gather(range(STEPS - 1))
 
+        def quantise_last_half(g):
+            nc.vector.quantize_mx(
+                out=xw_words[:, last, g, :].bitcast(FP8X4),
+                scales=xw_scales[:, last, g, :],
+                in_=grouped_of[last][:, g, :, :].rearrange("p b t -> p (b t)"),
+            )
+
+        quantise_last_half(0)
+        scores_of[last - 1] = compare(last - 1)
+        quantise_last_half(1)
+        scores_of[last] = compare(last)
+        for n in (last - 1, last):
+            sum_exponentials(n, scores_of[n])
+        gather(range(STEPS - 1))
+        spread(STEPS - 1, sum_exp, spread_sum)
+        for n in (last - 1, last):
+            finish_scores(n)
         gather(range(STEPS - 1, STEPS))
+
         log_sum = keep.tile([GROUPS, ROWS_PER_GROUP * N_PAIRS], F32)
         nc.scalar.activation(out=log_sum[:], in_=gathered["sum"][0:GROUPS, :], func=ACT.Ln)
         loss = keep.tile([GROUPS, ROWS_PER_GROUP * N_PAIRS], F32)
@@ -385,7 +406,8 @@ def tile_infonceloss_pa_e_kernel(tc, embeddings, contexts, W_words, W_scales, ou
         for step in range(STEPS):
             lo = first_pair[step]
             hi = lo + N_SLICES - step
-            nc.sync.dma_start(
+            queue = nc.sync if step % 2 == 0 else nc.scalar
+            queue.dma_start(
                 out=out[P * lo : P * hi].rearrange("(q r) -> q r", q=GROUPS),
                 in_=loss[:, ROWS_PER_GROUP * lo : ROWS_PER_GROUP * hi],
             )

@@ -156,15 +156,12 @@ def tile_infonceloss_pa_e_kernel(tc, embeddings, contexts, W_words, W_scales, ou
             op=ALU.add,
         )
 
-        def order_scales(slot, copy, pieces):
-            for h in range(D // K_PASS):
-                cols = slice(K_PASS * h, K_PASS * (h + 1))
-                for piece in range(pieces):
-                    ts = slice(PACK // pieces * piece, PACK // pieces * (piece + 1))
-                    copy(
-                        out=w_planes[:, slot, cols].rearrange("p (t m) -> p t m", t=PACK)[:, ts, :],
-                        in_=raw_planes[:, slot, cols].rearrange("p (m t) -> p t m", t=PACK)[:, ts, :],
-                    )
+        def order_scales(slot, h):
+            cols = slice(K_PASS * h, K_PASS * (h + 1))
+            nc.vector.tensor_copy(
+                out=w_planes[:, slot, cols].rearrange("p (t m) -> p t m", t=PACK),
+                in_=raw_planes[:, slot, cols].rearrange("p (m t) -> p t m", t=PACK),
+            )
 
         def order_weight(step, part):
             h, g = divmod(part, PASSES)
@@ -174,24 +171,17 @@ def tile_infonceloss_pa_e_kernel(tc, embeddings, contexts, W_words, W_scales, ou
                 in_=raw_words[:, step, g, cols].bitcast(I32).rearrange("p (m i t) -> p m t i", t=PACK, i=PACK),
             )
 
-        def part_words(raw, n):
-            parted = slice_stage.tile([P, PASSES, 2, P], I32, tag="parted", bufs=10)
-            words = raw[:, n, :].bitcast(I32).rearrange("b (g p u) -> b g u p", g=PASSES, u=2)
-            for g in range(PASSES):
-                nc.gpsimd.tensor_copy(out=parted[:, g, :, :], in_=words[:, g, :, :])
-            return parted
-
-        def turn_slice(raw, n, copy, parted=None):
+        def turn_slice(raw, n, copy):
             pairs_of_values = raw[:, n, :].bitcast(F32)
             words_per_pass = K_PASS // 2
             turned = psum_banks.tile([P, PASSES, 2, P], F32, tag="bank")
             for g in range(PASSES):
                 for u in range(2):
-                    if parted is None:
-                        words = pairs_of_values[:, words_per_pass * g + u : words_per_pass * (g + 1) : 2]
-                    else:
-                        words = parted[:, g, u, :].bitcast(F32)
-                    nc.tensor.transpose(turned[:, g, u, :], words, ident[:])
+                    nc.tensor.transpose(
+                        turned[:, g, u, :],
+                        pairs_of_values[:, words_per_pass * g + u : words_per_pass * (g + 1) : 2],
+                        ident[:],
+                    )
             grouped = slice_stage.tile([P, PASSES, P, PACK], BF16, tag="grouped", align_bytes=64)
             copy(out=grouped[:].bitcast(F32), in_=turned[:].rearrange("p g u b -> p g b u"))
             return grouped
@@ -209,12 +199,6 @@ def tile_infonceloss_pa_e_kernel(tc, embeddings, contexts, W_words, W_scales, ou
         def quantise_c(n, grouped):
             quantise(grouped, c_words[:, n, :, :], c_scales[:, n, :, :])
 
-        parted = {}
-        for turns in TURNS:
-            for kind, n in turns:
-                parted[kind, n] = part_words(e_raw if kind == "e" else c_raw, n)
-        for slot in range(1, n_slots):
-            order_scales(slot, nc.gpsimd.tensor_copy, 2)
         keep_warm(WARM_BEFORE)
         early = []
         for n in range(SLICES_AHEAD):
@@ -224,7 +208,8 @@ def tile_infonceloss_pa_e_kernel(tc, embeddings, contexts, W_words, W_scales, ou
         for n in range(SLICES_AHEAD):
             quantise_e(n, early[n])
             if n == 0:
-                order_scales(0, nc.vector.tensor_copy, 1)
+                for h in range(D // K_PASS):
+                    order_scales(0, h)
             if n % 2 == 1:
                 for part in range(PASSES):
                     order_weight(0, PASSES * (n // 2) + part)
@@ -367,6 +352,9 @@ def tile_infonceloss_pa_e_kernel(tc, embeddings, contexts, W_words, W_scales, ou
             if 0 < i <= len(TURNS):
                 for kind, n in TURNS[i - 1]:
                     (quantise_e if kind == "e" else quantise_c)(n, turned[kind, n])
+            if 0 <= i - first_pair[1] < (n_slots - 1) * (D // K_PASS):
+                slot, h = divmod(i - first_pair[1], D // K_PASS)
+                order_scales(1 + slot, h)
             for step in range(1, STEPS):
                 if 0 <= i - (first_pair[step] - W_PARTS) < W_PARTS:
                     order_weight(step, i - (first_pair[step] - W_PARTS))
@@ -378,7 +366,7 @@ def tile_infonceloss_pa_e_kernel(tc, embeddings, contexts, W_words, W_scales, ou
             if i < len(TURNS):
                 for place, (kind, n) in enumerate(TURNS[i]):
                     copy_out = nc.vector.tensor_copy if place == 1 else nc.scalar.copy
-                    turned[kind, n] = turn_slice(e_raw if kind == "e" else c_raw, n, copy_out, parted[kind, n])
+                    turned[kind, n] = turn_slice(e_raw if kind == "e" else c_raw, n, copy_out)
 
         def quantise_last_half(g):
             nc.vector.quantize_mx(

@@ -37,6 +37,7 @@ WARM_COLS = 512
 WARM_BEFORE = 7
 WARM_BETWEEN = 1
 WARM_AFTER = 2
+SCALES_ROUNDS = {1: (8, 8), 2: (17, 19)}
 W_PARTS = 4
 ROWS_PER_GROUP = 8
 GROUPS = P // ROWS_PER_GROUP
@@ -210,9 +211,9 @@ def tile_infonceloss_pa_e_kernel(tc, embeddings, contexts, W_words, W_scales, ou
             if n == 0:
                 for h in range(D // K_PASS):
                     order_scales(0, h)
-            if n % 2 == 1:
+            if n in (1, 2):
                 for part in range(PASSES):
-                    order_weight(0, PASSES * (n // 2) + part)
+                    order_weight(0, PASSES * (n - 1) + part)
 
         def project(i):
             step, s = pairs[i]
@@ -334,6 +335,11 @@ def tile_infonceloss_pa_e_kernel(tc, embeddings, contexts, W_words, W_scales, ou
         def quantise_pair(n):
             quantise(grouped_of[n], xw_words[:, n, :, :], xw_scales[:, n, :, :])
 
+        def words_round(step, part):
+            if step == 1:
+                return first_pair[1] - W_PARTS + part
+            return 4 * step + 2 + 2 * (part // 2)
+
         for i in range(N_PAIRS):
             if 0 <= i - EXP_LAG:
                 sum_exponentials(i - EXP_LAG, scores_of[i - EXP_LAG])
@@ -352,12 +358,14 @@ def tile_infonceloss_pa_e_kernel(tc, embeddings, contexts, W_words, W_scales, ou
             if 0 < i <= len(TURNS):
                 for kind, n in TURNS[i - 1]:
                     (quantise_e if kind == "e" else quantise_c)(n, turned[kind, n])
-            if 0 <= i - first_pair[1] < (n_slots - 1) * (D // K_PASS):
-                slot, h = divmod(i - first_pair[1], D // K_PASS)
-                order_scales(1 + slot, h)
             for step in range(1, STEPS):
-                if 0 <= i - (first_pair[step] - W_PARTS) < W_PARTS:
-                    order_weight(step, i - (first_pair[step] - W_PARTS))
+                for part in range(W_PARTS):
+                    if words_round(step, part) == i:
+                        order_weight(step, part)
+            for slot, rounds in SCALES_ROUNDS.items():
+                for h in range(D // K_PASS):
+                    if rounds[h] == i:
+                        order_scales(slot, h)
             if i == last:
                 for n in (last - COMPARE_LAG, last - 2):
                     finish_scores(n)

import math
from contextlib import ExitStack

import concourse.mybir as mybir
from concourse.masks import make_identity

F32 = mybir.dt.float32
BF16 = mybir.dt.bfloat16
I32 = mybir.dt.int32
U32 = mybir.dt.uint32
U8 = mybir.dt.uint8
FP8X4 = mybir.dt.float8_e4m3fn_x4
ALU = mybir.AluOpType
ACT = mybir.ActivationFunctionType
AXIS_X = mybir.AxisListType.X

P = 128
T = 8
N_SLICES = T - 1
D = 1024
STEPS = 5
PACK = 4
K_PASS = P * PACK
PASSES = D // K_PASS
PLANES_PER_SLOT = 4
QUADRANT = 32
SLICES_AHEAD = 4
TURNS = (
    (("e", 4), ("c", 0)),
    (("e", 5), ("c", 1)),
    (("e", 6), ("c", 2)),
    (("c", 3), ("c", 4)),
    (),
    (("c", 5), ("c", 6)),
)
WARM_COLS = 512
WARM_BEFORE = 7
WARM_BETWEEN = 1
WARM_AFTER = 2
SCALES_ROUNDS = {1: (8, 8), 2: (17, 19)}
W_PARTS = 4
ROWS_PER_GROUP = 8
GROUPS = P // ROWS_PER_GROUP
QUANTISE_LAG = 1
COMPARE_LAG = 3
EXP_LAG = 4

N_PAIRS = sum(N_SLICES - step for step in range(STEPS))
FLOPS = 2 * N_PAIRS * P * D * D + 2 * N_PAIRS * P * P * D


def tile_infonceloss_pa_e_kernel(tc, embeddings, contexts, W_words, W_scales, out):
    nc = tc.nc
    pairs = [(step, s) for step in range(STEPS) for s in range(N_SLICES - step)]
    first_pair = [pairs.index((step, 0)) for step in range(STEPS)]

    with ExitStack() as ctx:
        keep = ctx.enter_context(tc.tile_pool(name="keep", bufs=1))
        slice_stage = ctx.enter_context(tc.tile_pool(name="slice_stage", bufs=4))
        xw_stage = ctx.enter_context(tc.tile_pool(name="xw_stage", bufs=3))
        unread = ctx.enter_context(tc.tile_pool(name="unread", bufs=4))
        psum_banks = ctx.enter_context(tc.psum_pool(name="psum_banks", bufs=5))
        psum_scores = ctx.enter_context(tc.psum_pool(name="psum_scores", bufs=3))
        ctx.enter_context(tc.manual_schedule())

        e_raw = keep.tile([P, N_SLICES, D], BF16)
        c_raw = keep.tile([P, N_SLICES, D], BF16)
        w_words = keep.tile([P, STEPS, PASSES, D], U32, align_bytes=64)
        n_planes = STEPS * PASSES
        n_slots = (n_planes + PLANES_PER_SLOT - 1) // PLANES_PER_SLOT
        w_planes = keep.tile([P, n_slots, D], U8, align_bytes=64)
        raw_words = keep.tile([P, STEPS, PASSES, D], U32, align_bytes=64)
        raw_planes = keep.tile([P, n_slots, D], U8, align_bytes=64)
        e_words = keep.tile([P, N_SLICES, PASSES, P], U32, align_bytes=64)
        e_scales = keep.tile([P, N_SLICES, PASSES, P], U8, align_bytes=64)
        c_words = keep.tile([P, N_SLICES, PASSES, P], U32, align_bytes=64)
        c_scales = keep.tile([P, N_SLICES, PASSES, P], U8, align_bytes=64)
        xw_words = keep.tile([P, N_PAIRS, PASSES, P], U32, align_bytes=64)
        xw_scales = keep.tile([P, N_PAIRS, PASSES, P], U8, align_bytes=64)
        neg_max = keep.tile([P, N_PAIRS], F32)
        sum_exp = keep.tile([P, N_PAIRS], F32)
        diagonal = keep.tile([P, N_PAIRS], F32)
        shift = keep.tile([P, N_PAIRS], F32)
        spread_sum = keep.tile([P, ROWS_PER_GROUP * N_PAIRS], F32)
        spread_shift = keep.tile([P, ROWS_PER_GROUP * N_PAIRS], F32)

        def load_slice(source, raw, n, first_time):
            nc.sync.dma_start(out=raw[:, n, :], in_=source[:, first_time + n, :])

        def load_e(n):
            load_slice(embeddings, e_raw, n, 1)

        def load_c(n):
            load_slice(contexts, c_raw, n, 0)

        def load_scale_slot(slot):
            lo = PLANES_PER_SLOT * slot
            hi = min(lo + PLANES_PER_SLOT, n_planes)
            for quadrant in range(P // QUADRANT):
                top = QUADRANT * quadrant
                nc.sync.dma_start(
                    out=raw_planes[top : top + 4 * (hi - lo), slot, :].bitcast(I32),
                    in_=W_scales[lo:hi, 4 * quadrant : 4 * quadrant + 4, :].bitcast(I32),
                )

        def load_weight(step, lo, hi):
            nc.sync.dma_start(
                out=raw_words[:, step, :, lo:hi].bitcast(I32),
                in_=W_words[PASSES * step : PASSES * (step + 1)]
                .rearrange("g p n t -> p g (n t)")[:, :, PACK * lo : PACK * hi]
                .bitcast(I32),
            )

        zeros = keep.tile([P, WARM_COLS], BF16)
        nc.vector.memset(zeros[:].bitcast(I32), 0)
        warm_bank = psum_scores.tile([P, WARM_COLS], F32, tag="scores")

        def keep_warm(times):
            for turn in range(times):
                nc.tensor.matmul(out=warm_bank[:], lhsT=zeros[:, 0:P], rhs=zeros[:], start=True, stop=True)

        nc.vector.memset(raw_planes[:, 0, :].bitcast(I32), 0)
        nc.vector.memset(raw_planes[:, 1:n_slots, :].bitcast(I32), 0)

        load_e(0)
        load_scale_slot(0)
        for n in range(1, SLICES_AHEAD):
            load_e(n)
        load_weight(0, 0, K_PASS)
        load_weight(0, K_PASS, D)
        for i, turns in enumerate(TURNS):
            if i == first_pair[1] - W_PARTS + 1:
                load_weight(1, 0, D)
            for kind, n in turns:
                (load_e if kind == "e" else load_c)(n)
        load_weight(2, 0, D)
        for slot in range(1, n_slots):
            load_scale_slot(slot)
        for step in range(3, STEPS):
            load_weight(step, 0, D)

        ident = keep.tile([P, P], F32)
        make_identity(nc, ident[:])
        group_of_row = keep.tile([P, P], F32)
        nc.vector.memset(group_of_row[:], 0.0)
        nc.vector.tensor_reduce(
            out=group_of_row[:, 0:GROUPS],
            in_=ident[:].rearrange("p (q i) -> p q i", i=ROWS_PER_GROUP),
            axis=AXIS_X,
            op=ALU.add,
        )
        place_in_group = keep.tile([P, ROWS_PER_GROUP], F32)
        nc.vector.tensor_reduce(
            out=place_in_group[:],
            in_=ident[:].rearrange("p (q i) -> p i q", i=ROWS_PER_GROUP),
            axis=AXIS_X,
            op=ALU.add,
        )

        def order_scales(slot, h):
            cols = slice(K_PASS * h, K_PASS * (h + 1))
            nc.vector.tensor_copy(
                out=w_planes[:, slot, cols].rearrange("p (t m) -> p t m", t=PACK),
                in_=raw_planes[:, slot, cols].rearrange("p (m t) -> p t m", t=PACK),
            )

        def order_weight(step, part):
            h, g = divmod(part, PASSES)
            cols = slice(K_PASS * h, K_PASS * (h + 1))
            nc.vector.tensor_copy(
                out=w_words[:, step, g, cols].bitcast(I32).rearrange("p (t m i) -> p m t i", t=PACK, i=PACK),
                in_=raw_words[:, step, g, cols].bitcast(I32).rearrange("p (m i t) -> p m t i", t=PACK, i=PACK),
            )

        def turn_slice(raw, n, copy):
            pairs_of_values = raw[:, n, :].bitcast(F32)
            words_per_pass = K_PASS // 2
            turned = psum_banks.tile([P, PASSES, 2, P], F32, tag="bank")
            for g in range(PASSES):
                for u in range(2):
                    nc.tensor.transpose(
                        turned[:, g, u, :],
                        pairs_of_values[:, words_per_pass * g + u : words_per_pass * (g + 1) : 2],
                        ident[:],
                    )
            grouped = slice_stage.tile([P, PASSES, P, PACK], BF16, tag="grouped", align_bytes=64)
            copy(out=grouped[:].bitcast(F32), in_=turned[:].rearrange("p g u b -> p g b u"))
            return grouped

        def quantise(grouped, words, scales):
            nc.vector.quantize_mx(
                out=words.rearrange("p g b -> p (g b)").bitcast(FP8X4),
                scales=scales.rearrange("p g b -> p (g b)"),
                in_=grouped[:].rearrange("p g b t -> p (g b t)"),
            )

        def quantise_e(n, grouped):
            quantise(grouped, e_words[:, n, :, :], e_scales[:, n, :, :])

        def quantise_c(n, grouped):
            quantise(grouped, c_words[:, n, :, :], c_scales[:, n, :, :])

        keep_warm(WARM_BEFORE)
        early = []
        for n in range(SLICES_AHEAD):
            early.append(turn_slice(e_raw, n, nc.scalar.copy))
            keep_warm(WARM_BETWEEN)
        keep_warm(WARM_AFTER)
        for n in range(SLICES_AHEAD):
            quantise_e(n, early[n])
            if n == 0:
                for h in range(D // K_PASS):
                    order_scales(0, h)
            if n in (1, 2):
                for part in range(PASSES):
                    order_weight(0, PASSES * (n - 1) + part)

        def project(i):
            step, s = pairs[i]
            grouped = xw_stage.tile([P, PASSES, P, PACK], BF16, tag="xw_grouped", align_bytes=64)
            for g in range(PASSES):
                bank = psum_banks.tile([P, PACK, P], F32, tag="bank")
                for t in range(PACK):
                    lo = K_PASS * g + P * t
                    for k_pass in range(PASSES):
                        slot, place = divmod(PASSES * step + k_pass, PLANES_PER_SLOT)
                        nc.tensor.matmul_mx(
                            out=bank[:, t, :],
                            lhsT=w_words[:, step, k_pass, lo : lo + P].bitcast(FP8X4),
                            lhsT_scale=w_planes[4 * place : P, slot, lo : lo + P],
                            rhs=e_words[:, step + s, k_pass, :].bitcast(FP8X4),
                            rhs_scale=e_scales[:, step + s, k_pass, :],
                            start=(k_pass == 0),
                            stop=(k_pass == PASSES - 1),
                        )
                to_vector = step > 0 and i % 2 == 1 and i < N_PAIRS - 2 and g == PASSES - 1
                copy_out = nc.vector.tensor_copy if to_vector else nc.scalar.copy
                copy_out(out=grouped[:, g, :, :], in_=bank[:].rearrange("p t b -> p b t"))
            return grouped

        def compare(i):
            step, s = pairs[i]
            pool, tag = (psum_scores, "scores") if i < N_PAIRS - 2 else (psum_banks, "bank")
            scores = pool.tile([P, P], F32, tag=tag)
            for g in range(PASSES):
                nc.tensor.matmul_mx(
                    out=scores[:],
                    lhsT=xw_words[:, i, g, :].bitcast(FP8X4),
                    lhsT_scale=xw_scales[:, i, g, :],
                    rhs=c_words[:, s, g, :].bitcast(FP8X4),
                    rhs_scale=c_scales[:, s, g, :],
                    start=(g == 0),
                    stop=(g == PASSES - 1),
                )
            nc.vector.tensor_reduce(out=neg_max[:, i : i + 1], in_=scores[:], axis=AXIS_X, op=ALU.max, negate=True)
            return scores

        def take_diagonal(i, scores):
            masked = unread.tile([P, P], F32, tag="masked")
            nc.vector.scalar_tensor_tensor(
                out=masked[:],
                in0=scores[:],
                scalar=1.0,
                in1=ident[:],
                op0=ALU.mult,
                op1=ALU.mult,
                accum_out=diagonal[:, i : i + 1],
            )

        def sum_exponentials(i, scores):
            exponentials = unread.tile([P, P], F32, tag="exponentials")
            nc.scalar.activation(
                out=exponentials[:],
                in_=scores[:],
                func=ACT.Exp,
                bias=neg_max[:, i : i + 1],
                scale=1.0,
                accum_out=sum_exp[:, i : i + 1],
            )

        def spread(step, values, spread_tile):
            n_times = N_SLICES - step
            lo = first_pair[step]
            shape = [P, ROWS_PER_GROUP, n_times]
            nc.vector.tensor_tensor(
                out=spread_tile[:, ROWS_PER_GROUP * lo : ROWS_PER_GROUP * (lo + n_times)].rearrange(
                    "p (i s) -> p i s", s=n_times
                ),
                in0=values[:, lo : lo + n_times].unsqueeze(1).to_broadcast(shape),
                in1=place_in_group[:].unsqueeze(2).to_broadcast(shape),
                op=ALU.mult,
            )

        def spread_shift_of(step):
            n_times = N_SLICES - step
            lo = first_pair[step]
            nc.vector.scalar_tensor_tensor(
                out=shift[:, lo : lo + n_times],
                in0=neg_max[:, lo : lo + n_times],
                scalar=math.log(P * n_times),
                in1=diagonal[:, lo : lo + n_times],
                op0=ALU.add,
                op1=ALU.add,
            )
            spread(step, shift, spread_shift)

        gathered = {}

        def gather(steps):
            if not gathered:
                for name in ("shift", "sum"):
                    bank = psum_banks.tile([P, ROWS_PER_GROUP * N_PAIRS], F32, tag="bank")
                    gathered[name] = bank
            lo = ROWS_PER_GROUP * first_pair[steps[0]]
            hi = ROWS_PER_GROUP * (first_pair[steps[-1]] + N_SLICES - steps[-1])
            for name, values in (("sum", spread_sum), ("shift", spread_shift)):
                nc.tensor.matmul(
                    out=gathered[name][:, lo:hi], lhsT=group_of_row[:], rhs=values[:, lo:hi], start=True, stop=True
                )

        def ends_step(i):
            step, s = pairs[i]
            return s == N_SLICES - step - 1

        last = N_PAIRS - 1
        grouped_of = {}
        scores_of = {}
        turned = {}

        def finish_scores(n):
            take_diagonal(n, scores_of[n])
            if ends_step(n):
                spread_shift_of(pairs[n][0])

        def quantise_pair(n):
            quantise(grouped_of[n], xw_words[:, n, :, :], xw_scales[:, n, :, :])

        def words_round(step, part):
            if step == 1:
                return first_pair[1] - W_PARTS + part
            return 4 * step + 2 + 2 * (part // 2)

        for i in range(N_PAIRS):
            if 0 <= i - EXP_LAG:
                sum_exponentials(i - EXP_LAG, scores_of[i - EXP_LAG])
            if 0 <= i - COMPARE_LAG:
                scores_of[i - COMPARE_LAG] = compare(i - COMPARE_LAG)
                if i < last:
                    finish_scores(i - COMPARE_LAG)
            if i == last:
                scores_of[last - 2] = compare(last - 2)
                for n in (last - COMPARE_LAG, last - 2):
                    sum_exponentials(n, scores_of[n])
            if i >= 1:
                quantise_pair(i - 1)
            if 0 <= i - EXP_LAG and ends_step(i - EXP_LAG):
                spread(pairs[i - EXP_LAG][0], sum_exp, spread_sum)
            if 0 < i <= len(TURNS):
                for kind, n in TURNS[i - 1]:
                    (quantise_e if kind == "e" else quantise_c)(n, turned[kind, n])
            for step in range(1, STEPS):
                for part in range(W_PARTS):
                    if words_round(step, part) == i:
                        order_weight(step, part)
            for slot, rounds in SCALES_ROUNDS.items():
                for h in range(D // K_PASS):
                    if rounds[h] == i:
                        order_scales(slot, h)
            if i == last:
                for n in (last - COMPARE_LAG, last - 2):
                    finish_scores(n)
                spread(STEPS - 2, sum_exp, spread_sum)
            grouped_of[i] = project(i)
            if i < len(TURNS):
                for place, (kind, n) in enumerate(TURNS[i]):
                    copy_out = nc.vector.tensor_copy if place == 1 else nc.scalar.copy
                    turned[kind, n] = turn_slice(e_raw if kind == "e" else c_raw, n, copy_out)

        def quantise_last_half(g):
            nc.vector.quantize_mx(
                out=xw_words[:, last, g, :].bitcast(FP8X4),
                scales=xw_scales[:, last, g, :],
                in_=grouped_of[last][:, g, :, :].rearrange("p b t -> p (b t)"),
            )

        quantise_last_half(0)
        scores_of[last - 1] = compare(last - 1)
        quantise_last_half(1)
        scores_of[last] = compare(last)
        for n in (last - 1, last):
            sum_exponentials(n, scores_of[n])
        gather(range(STEPS - 1))
        spread(STEPS - 1, sum_exp, spread_sum)
        for n in (last - 1, last):
            finish_scores(n)
        gather(range(STEPS - 1, STEPS))

        log_sum = keep.tile([GROUPS, ROWS_PER_GROUP * N_PAIRS], F32)
        nc.scalar.activation(out=log_sum[:], in_=gathered["sum"][0:GROUPS, :], func=ACT.Ln)
        loss = keep.tile([GROUPS, ROWS_PER_GROUP * N_PAIRS], F32)
        nc.vector.tensor_tensor(out=loss[:], in0=log_sum[:], in1=gathered["shift"][0:GROUPS, :], op=ALU.subtract)
        for step in range(STEPS):
            lo = first_pair[step]
            hi = lo + N_SLICES - step
            queue = nc.sync if step % 2 == 0 else nc.scalar
            queue.dma_start(
                out=out[P * lo : P * hi].rearrange("(q r) -> q r", q=GROUPS),
                in_=loss[:, ROWS_PER_GROUP * lo : ROWS_PER_GROUP * hi],
            )
